import numpy as np
import ml_dtypes


def mxq(x, axis, fmt="e4m3"):
    dtype, down = {"e4m3": (ml_dtypes.float8_e4m3fn, 7), "e5m2": (ml_dtypes.float8_e5m2, 14)}[fmt]
    v = np.moveaxis(np.asarray(x, np.float32).astype(ml_dtypes.bfloat16).astype(np.float64), axis, -1)
    blocks = v.reshape(v.shape[:-1] + (-1, 32))
    amax = np.abs(blocks).max(-1, keepdims=True)
    byte = np.maximum(np.where(amax > 0, np.frexp(amax)[1] - 1 + 127, 0) - down, 1)
    scale = np.exp2(byte - 127.0)
    codes = (blocks / scale).astype(np.float32).astype(dtype).astype(np.float64)
    return np.moveaxis((codes * scale).reshape(v.shape), -1, axis)


WIDE = False


def mx_kscale(k):
    if not WIDE:
        return np.ones(k)
    levels = np.array([10, -10, 5, -5, 0])
    a = np.random.permutation(np.resize(levels, k // 512 * 4)).reshape(k // 512, 4)
    idx = np.arange(k)
    return np.exp2(a[idx // 512, idx % 128 // 32])


BF16 = ml_dtypes.bfloat16


def bf(x):
    return np.asarray(x, np.float32).astype(BF16)


def f64(x):
    return np.asarray(x).astype(np.float64)


B, N, D0, D1, D2, D3 = 64, 128, 512, 512, 512, 1024
EPS = 1e-5


def batch_norm(x, g, b):
    mean = x.mean(axis=(0, 1))
    var = np.square(x - mean).mean(axis=(0, 1))
    return (x - mean) * (1.0 / np.sqrt(var + EPS)) * g + b


def setup_inputs():
    s = mx_kscale(D0)
    feats = np.random.standard_normal((B, N, D0)) * np.exp(0.4 * np.random.standard_normal(D0)) + 0.5 * np.random.standard_normal(D0)
    return {"set_feats": bf(feats),
            "g0": bf((1.0 + 0.2 * np.random.standard_normal(D0)) * s),
            "b0": bf(0.2 * np.random.standard_normal(D0) * s),
            "W0": bf(np.random.standard_normal((D1, D0)) / np.sqrt(D0) / s),
            "c0": bf(0.3 * np.random.standard_normal(D1)),
            "g1": bf(1.0 + 0.2 * np.random.standard_normal(D1)),
            "b1": bf(0.2 * np.random.standard_normal(D1))}


def reference(set_feats, g0, b0, W0, c0, g1, b1):
    x0 = batch_norm(f64(set_feats), f64(g0), f64(b0))
    h0 = np.maximum((mxq(x0, 2, "e4m3") @ mxq(f64(W0), 1, "e4m3").T) + f64(c0), 0.0)
    return batch_norm(h0, f64(g1), f64(b1))

@@ -1,0 +1,224 @@
+import concourse.mybir as mybir
+from concourse.masks import make_identity
+
+F32 = mybir.dt.float32
+BF16 = mybir.dt.bfloat16
+U32 = mybir.dt.uint32
+U8 = mybir.dt.uint8
+FP8X4 = mybir.dt.float8_e4m3fn_x4
+ALU = mybir.AluOpType
+FUNC = mybir.ActivationFunctionType
+
+P = 128
+PACK = 4
+ROWS = 64 * 128
+D_IN = 512
+D_OUT = 512
+EPS = 1e-5
+BLOCKS = 4
+ROWS_PER_PARTITION = ROWS // P
+CHUNK = 512
+SLICES = CHUNK // P
+CHUNKS = ROWS // CHUNK
+SLICES_PER_LOAD = 8
+LOADS = ROWS_PER_PARTITION // SLICES_PER_LOAD
+STATS = 6
+VECTOR_REGROUPS_EVERY = 4
+
+FLOPS = 2 * ROWS * D_IN * D_OUT
+
+
+def norm_coefficients(nc, pool, stats, gain, shift, label):
+    mean_var = pool.tile([P, BLOCKS, 2], F32, name=label + "_mean_var")
+    for block in range(BLOCKS):
+        nc.vector.bn_aggr(
+            out=mean_var[:, block, :],
+            in_=stats[:, block, :, :].rearrange("p j s -> p (j s)"),
+        )
+    mean = mean_var[:, :, 0]
+    var_eps = pool.tile([P, BLOCKS], F32, name=label + "_var_eps")
+    nc.vector.tensor_scalar_add(out=var_eps[:], in0=mean_var[:, :, 1], scalar1=EPS)
+    rstd = pool.tile([P, BLOCKS], F32, name=label + "_rstd")
+    nc.scalar.sqrt(out=rstd[:], in_=var_eps[:])
+    nc.vector.reciprocal(out=rstd[:], in_=rstd[:])
+    newton = pool.tile([P, BLOCKS], F32, name=label + "_newton")
+    nc.vector.tensor_mul(out=newton[:], in0=rstd[:], in1=rstd[:])
+    nc.vector.tensor_mul(out=newton[:], in0=newton[:], in1=var_eps[:])
+    nc.vector.tensor_scalar(
+        out=newton[:], in0=newton[:], scalar1=-0.5, scalar2=1.5, op0=ALU.mult, op1=ALU.add
+    )
+    nc.vector.tensor_mul(out=rstd[:], in0=rstd[:], in1=newton[:])
+    scale = pool.tile([P, BLOCKS], F32, name=label + "_scale")
+    nc.vector.tensor_mul(out=scale[:], in0=rstd[:], in1=gain)
+    offset = pool.tile([P, BLOCKS], F32, name=label + "_offset")
+    nc.vector.tensor_mul(out=offset[:], in0=mean, in1=scale[:])
+    nc.vector.tensor_sub(out=offset[:], in0=shift, in1=offset[:])
+    return scale, offset
+
+
+def tile_settransform_pa_kernel(tc, set_feats, g0, b0, W0, c0, g1, b1, out):
+    nc = tc.nc
+    x_rows = set_feats.flatten_outer_dims().rearrange("(p c) k -> p c k", c=ROWS_PER_PARTITION)
+    out_rows = out.flatten_outer_dims().rearrange("(p c) f -> p c f", c=ROWS_PER_PARTITION)
+
+    with tc.tile_pool(name="keep", bufs=1) as keep:
+        ident_bf16 = keep.tile([P, P], BF16, name="ident_bf16")
+        make_identity(nc, ident_bf16[:])
+        ident_f32 = keep.tile([P, P], F32, name="ident_f32")
+        make_identity(nc, ident_f32[:])
+        warm = keep.tile([P, 1], F32, name="warm")
+        nc.vector.memset(warm[:], 1.0)
+        nc.scalar.sqrt(out=warm[:], in_=warm[:])
+
+        w_codes = keep.tile([P, D_OUT], U32, name="w_codes", align_bytes=64)
+        w_scales = keep.tile([P, D_OUT], U8, name="w_scales", align_bytes=64)
+        params = keep.tile([P, 5 * BLOCKS], F32, name="params")
+        stats0 = keep.tile([P, BLOCKS, CHUNKS, STATS], F32, name="stats0")
+        stats1 = keep.tile([P, BLOCKS, CHUNKS, STATS], F32, name="stats1")
+        xt = [keep.tile([P, BLOCKS, CHUNK], BF16, name="xt%d" % j) for j in range(CHUNKS)]
+
+        with tc.tile_pool(name="natural", bufs=1) as natural, tc.psum_pool(
+            name="turned", bufs=6
+        ) as turned_pool:
+            w_nat = natural.tile([P, BLOCKS, D_IN], BF16, name="w_nat")
+            nc.scalar.dma_start(out=w_nat[:], in_=W0.rearrange("(b f) k -> f b k", f=P))
+            vec_rows = natural.tile([P, P], BF16, name="vec_rows")
+            nc.vector.memset(vec_rows[:], 0.0)
+            for v, vec in enumerate((g0, b0, c0, g1, b1)):
+                nc.scalar.dma_start(
+                    out=vec_rows[BLOCKS * v : BLOCKS * (v + 1), :],
+                    in_=vec.rearrange("(t p) -> t p", p=P),
+                )
+            x_nat = []
+            for load in range(LOADS):
+                x_load = natural.tile([P, SLICES_PER_LOAD, D_IN], BF16, name="x_load%d" % load)
+                first = load * SLICES_PER_LOAD
+                nc.sync.dma_start(out=x_load[:], in_=x_rows[:, first : first + SLICES_PER_LOAD, :])
+                x_nat.append(x_load)
+
+            vec_turned = turned_pool.tile([P, PACK, P], BF16, tag="turned")
+            nc.tensor.transpose(out=vec_turned[:, 0, :], in_=vec_rows[:], identity=ident_bf16[:])
+            nc.vector.tensor_copy(out=params[:], in_=vec_turned[:, 0, 0 : 5 * BLOCKS])
+
+            w_grouped = natural.tile([P, D_OUT, PACK], BF16, name="w_grouped", align_bytes=64)
+            for block in range(BLOCKS):
+                w_turned = turned_pool.tile([P, PACK, P], BF16, tag="turned")
+                for t in range(PACK):
+                    nc.tensor.transpose(
+                        out=w_turned[:, t, :],
+                        in_=w_nat[:, block, t * P : (t + 1) * P],
+                        identity=ident_bf16[:],
+                    )
+                nc.scalar.copy(
+                    out=w_grouped[:, block * P : (block + 1) * P, :],
+                    in_=w_turned[:].rearrange("p t f -> p f t"),
+                )
+            nc.vector.quantize_mx(
+                out=w_codes[:].bitcast(FP8X4),
+                scales=w_scales[:],
+                in_=w_grouped[:].rearrange("p f t -> p (f t)"),
+            )
+
+            for j in range(CHUNKS):
+                for s in range(SLICES):
+                    c = j * SLICES + s
+                    x_slice = x_nat[c // SLICES_PER_LOAD][:, c % SLICES_PER_LOAD, :]
+                    x_turned = turned_pool.tile([P, PACK, P], BF16, tag="turned")
+                    for t in range(PACK):
+                        nc.tensor.transpose(
+                            out=x_turned[:, t, :],
+                            in_=x_slice[:, t * P : (t + 1) * P],
+                            identity=ident_bf16[:],
+                        )
+                    nc.scalar.copy(out=xt[j][:, :, s * P : (s + 1) * P], in_=x_turned[:])
+                for t in range(PACK):
+                    nc.vector.bn_stats(out=stats0[:, t, j, :], in_=xt[j][:, t, :])
+
+        scale0, offset0 = norm_coefficients(
+            nc, keep, stats0, params[:, 0:BLOCKS], params[:, BLOCKS : 2 * BLOCKS], "norm0"
+        )
+        bias = params[:, 2 * BLOCKS : 3 * BLOCKS]
+
+        with tc.tile_pool(name="hidden", bufs=1) as hidden:
+            h = [hidden.tile([P, BLOCKS, CHUNK], F32, name="h%d" % j) for j in range(CHUNKS)]
+
+            with tc.tile_pool(name="operand", bufs=3) as operand, tc.psum_pool(
+                name="sums", bufs=8
+            ) as sums_pool:
+                for j in range(CHUNKS):
+                    for t in range(PACK):
+                        nc.vector.tensor_scalar(
+                            out=xt[j][:, t, :],
+                            in0=xt[j][:, t, :],
+                            scalar1=scale0[:, t : t + 1],
+                            scalar2=offset0[:, t : t + 1],
+                            op0=ALU.mult,
+                            op1=ALU.add,
+                        )
+                    grouped = operand.tile([P, CHUNK, PACK], BF16, name="grouped", align_bytes=64)
+                    grouped_view = grouped[:].rearrange("p (c i) t -> p c t i", i=4)
+                    planes_view = xt[j][:].rearrange("p t (c i) -> p c t i", i=4)
+                    if j % VECTOR_REGROUPS_EVERY == 0:
+                        nc.vector.tensor_copy(out=grouped_view, in_=planes_view)
+                    else:
+                        nc.scalar.copy(out=grouped_view, in_=planes_view)
+                    codes = operand.tile([P, CHUNK], U32, name="codes", align_bytes=64)
+                    scales = operand.tile([P, CHUNK], U8, name="scales", align_bytes=64)
+                    nc.vector.quantize_mx(
+                        out=codes[:].bitcast(FP8X4),
+                        scales=scales[:],
+                        in_=grouped[:].rearrange("p n t -> p (n t)"),
+                    )
+                    for block in range(BLOCKS):
+                        features = slice(block * P, (block + 1) * P)
+                        sums = sums_pool.tile([P, CHUNK], F32, name="sums")
+                        nc.tensor.matmul_mx(
+                            out=sums[:],
+                            lhsT=w_codes[:, features].bitcast(FP8X4),
+                            lhsT_scale=w_scales[:, features],
+                            rhs=codes[:].bitcast(FP8X4),
+                            rhs_scale=scales[:],
+                            start=True,
+                            stop=True,
+                        )
+                        nc.scalar.activation(
+                            out=h[j][:, block, :],
+                            in_=sums[:],
+                            func=FUNC.Relu,
+                            bias=bias[:, block : block + 1],
+                        )
+                        nc.vector.bn_stats(out=stats1[:, block, j, :], in_=h[j][:, block, :])
+
+            scale1, offset1 = norm_coefficients(
+                nc, keep, stats1, params[:, 3 * BLOCKS : 4 * BLOCKS], params[:, 4 * BLOCKS :], "norm1"
+            )
+
+            with tc.tile_pool(name="result", bufs=3) as result_pool, tc.psum_pool(
+                name="back", bufs=8
+            ) as back_pool:
+                for j in range(CHUNKS):
+                    for block in range(BLOCKS):
+                        nc.vector.tensor_scalar(
+                            out=h[j][:, block, :],
+                            in0=h[j][:, block, :],
+                            scalar1=scale1[:, block : block + 1],
+                            scalar2=offset1[:, block : block + 1],
+                            op0=ALU.mult,
+                            op1=ALU.add,
+                        )
+                    result = result_pool.tile([P, SLICES, D_OUT], F32, name="result")
+                    for s in range(SLICES):
+                        back = back_pool.tile([P, D_OUT], F32, name="back")
+                        for block in range(BLOCKS):
+                            nc.tensor.transpose(
+                                out=back[:, block * P : (block + 1) * P],
+                                in_=h[j][:, block, s * P : (s + 1) * P],
+                                identity=ident_f32[:],
+                            )
+                        if s == SLICES - 1:
+                            nc.vector.tensor_copy(out=result[:, s, :], in_=back[:])
+                        else:
+                            nc.scalar.copy(out=result[:, s, :], in_=back[:])
+                    nc.sync.dma_start(
+                        out=out_rows[:, j * SLICES : (j + 1) * SLICES, :], in_=result[:]
+                    )

@@ -20,21 +20,15 @@ ROWS_PER_PARTITION = ROWS // P
 CHUNK = 512
 SLICES = CHUNK // P
 CHUNKS = ROWS // CHUNK
-SLICES_PER_LOAD = 8
-LOADS = ROWS_PER_PARTITION // SLICES_PER_LOAD
 STATS = 6
-VECTOR_REGROUPS_EVERY = 4
+CHUNKS_BEFORE_W = 2
+VECTOR_BLOCKS = 2
+SCALAR_BLOCKS = BLOCKS - VECTOR_BLOCKS
 
 FLOPS = 2 * ROWS * D_IN * D_OUT
 
 
-def norm_coefficients(nc, pool, stats, gain, shift, label):
-    mean_var = pool.tile([P, BLOCKS, 2], F32, name=label + "_mean_var")
-    for block in range(BLOCKS):
-        nc.vector.bn_aggr(
-            out=mean_var[:, block, :],
-            in_=stats[:, block, :, :].rearrange("p j s -> p (j s)"),
-        )
+def norm_coefficients(nc, pool, mean_var, gain, shift, label):
     mean = mean_var[:, :, 0]
     var_eps = pool.tile([P, BLOCKS], F32, name=label + "_var_eps")
     nc.vector.tensor_scalar_add(out=var_eps[:], in0=mean_var[:, :, 1], scalar1=EPS)
@@ -74,14 +68,23 @@ def tile_settransform_pa_kernel(tc, set_feats, g0, b0, W0, c0, g1, b1, out):
         w_scales = keep.tile([P, D_OUT], U8, name="w_scales", align_bytes=64)
         params = keep.tile([P, 5 * BLOCKS], F32, name="params")
         stats0 = keep.tile([P, BLOCKS, CHUNKS, STATS], F32, name="stats0")
-        stats1 = keep.tile([P, BLOCKS, CHUNKS, STATS], F32, name="stats1")
+        stats1 = keep.tile([P, VECTOR_BLOCKS, CHUNKS, STATS], F32, name="stats1")
+        sum_h = keep.tile([P, SCALAR_BLOCKS, CHUNKS], F32, name="sum_h")
+        sum_sq = keep.tile([P, SCALAR_BLOCKS, CHUNKS], F32, name="sum_sq")
+        neg_shift = keep.tile([P, SCALAR_BLOCKS], F32, name="neg_shift")
         xt = [keep.tile([P, BLOCKS, CHUNK], BF16, name="xt%d" % j) for j in range(CHUNKS)]
 
         with tc.tile_pool(name="natural", bufs=1) as natural, tc.psum_pool(
             name="turned", bufs=6
         ) as turned_pool:
+            x_nat = [natural.tile([P, SLICES, D_IN], BF16, name="x_nat%d" % j) for j in range(CHUNKS)]
             w_nat = natural.tile([P, BLOCKS, D_IN], BF16, name="w_nat")
-            nc.scalar.dma_start(out=w_nat[:], in_=W0.rearrange("(b f) k -> f b k", f=P))
+            for j in range(CHUNKS):
+                if j == CHUNKS_BEFORE_W:
+                    nc.sync.dma_start(out=w_nat[:], in_=W0.rearrange("(b f) k -> f b k", f=P))
+                nc.sync.dma_start(
+                    out=x_nat[j][:], in_=x_rows[:, j * SLICES : (j + 1) * SLICES, :]
+                )
             vec_rows = natural.tile([P, P], BF16, name="vec_rows")
             nc.vector.memset(vec_rows[:], 0.0)
             for v, vec in enumerate((g0, b0, c0, g1, b1)):
@@ -89,53 +92,53 @@ def tile_settransform_pa_kernel(tc, set_feats, g0, b0, W0, c0, g1, b1, out):
                     out=vec_rows[BLOCKS * v : BLOCKS * (v + 1), :],
                     in_=vec.rearrange("(t p) -> t p", p=P),
                 )
-            x_nat = []
-            for load in range(LOADS):
-                x_load = natural.tile([P, SLICES_PER_LOAD, D_IN], BF16, name="x_load%d" % load)
-                first = load * SLICES_PER_LOAD
-                nc.sync.dma_start(out=x_load[:], in_=x_rows[:, first : first + SLICES_PER_LOAD, :])
-                x_nat.append(x_load)
-
-            vec_turned = turned_pool.tile([P, PACK, P], BF16, tag="turned")
-            nc.tensor.transpose(out=vec_turned[:, 0, :], in_=vec_rows[:], identity=ident_bf16[:])
-            nc.vector.tensor_copy(out=params[:], in_=vec_turned[:, 0, 0 : 5 * BLOCKS])
-
-            w_grouped = natural.tile([P, D_OUT, PACK], BF16, name="w_grouped", align_bytes=64)
-            for block in range(BLOCKS):
-                w_turned = turned_pool.tile([P, PACK, P], BF16, tag="turned")
-                for t in range(PACK):
-                    nc.tensor.transpose(
-                        out=w_turned[:, t, :],
-                        in_=w_nat[:, block, t * P : (t + 1) * P],
-                        identity=ident_bf16[:],
-                    )
-                nc.scalar.copy(
-                    out=w_grouped[:, block * P : (block + 1) * P, :],
-                    in_=w_turned[:].rearrange("p t f -> p f t"),
-                )
-            nc.vector.quantize_mx(
-                out=w_codes[:].bitcast(FP8X4),
-                scales=w_scales[:],
-                in_=w_grouped[:].rearrange("p f t -> p (f t)"),
-            )
 
             for j in range(CHUNKS):
+                if j == CHUNKS_BEFORE_W:
+                    w_grouped = natural.tile(
+                        [P, D_OUT, PACK], BF16, name="w_grouped", align_bytes=64
+                    )
+                    for block in range(BLOCKS):
+                        w_turned = turned_pool.tile([P, PACK, P], BF16, tag="turned")
+                        for t in range(PACK):
+                            nc.tensor.transpose(
+                                out=w_turned[:, t, :],
+                                in_=w_nat[:, block, t * P : (t + 1) * P],
+                                identity=ident_bf16[:],
+                            )
+                        nc.scalar.copy(
+                            out=w_grouped[:, block * P : (block + 1) * P, :],
+                            in_=w_turned[:].rearrange("p t f -> p f t"),
+                        )
+                    nc.vector.quantize_mx(
+                        out=w_codes[:].bitcast(FP8X4),
+                        scales=w_scales[:],
+                        in_=w_grouped[:].rearrange("p f t -> p (f t)"),
+                    )
+                    vec_turned = turned_pool.tile([P, PACK, P], BF16, tag="turned")
+                    nc.tensor.transpose(
+                        out=vec_turned[:, 0, :], in_=vec_rows[:], identity=ident_bf16[:]
+                    )
+                    nc.vector.tensor_copy(out=params[:], in_=vec_turned[:, 0, 0 : 5 * BLOCKS])
                 for s in range(SLICES):
-                    c = j * SLICES + s
-                    x_slice = x_nat[c // SLICES_PER_LOAD][:, c % SLICES_PER_LOAD, :]
                     x_turned = turned_pool.tile([P, PACK, P], BF16, tag="turned")
                     for t in range(PACK):
                         nc.tensor.transpose(
                             out=x_turned[:, t, :],
-                            in_=x_slice[:, t * P : (t + 1) * P],
+                            in_=x_nat[j][:, s, t * P : (t + 1) * P],
                             identity=ident_bf16[:],
                         )
                     nc.scalar.copy(out=xt[j][:, :, s * P : (s + 1) * P], in_=x_turned[:])
                 for t in range(PACK):
                     nc.vector.bn_stats(out=stats0[:, t, j, :], in_=xt[j][:, t, :])
 
+        mean_var0 = keep.tile([P, BLOCKS, 2], F32, name="mean_var0")
+        for t in range(PACK):
+            nc.vector.bn_aggr(
+                out=mean_var0[:, t, :], in_=stats0[:, t, :, :].rearrange("p j s -> p (j s)")
+            )
         scale0, offset0 = norm_coefficients(
-            nc, keep, stats0, params[:, 0:BLOCKS], params[:, BLOCKS : 2 * BLOCKS], "norm0"
+            nc, keep, mean_var0, params[:, 0:BLOCKS], params[:, BLOCKS : 2 * BLOCKS], "norm0"
         )
         bias = params[:, 2 * BLOCKS : 3 * BLOCKS]
 
@@ -158,10 +161,7 @@ def tile_settransform_pa_kernel(tc, set_feats, g0, b0, W0, c0, g1, b1, out):
                     grouped = operand.tile([P, CHUNK, PACK], BF16, name="grouped", align_bytes=64)
                     grouped_view = grouped[:].rearrange("p (c i) t -> p c t i", i=4)
                     planes_view = xt[j][:].rearrange("p t (c i) -> p c t i", i=4)
-                    if j % VECTOR_REGROUPS_EVERY == 0:
-                        nc.vector.tensor_copy(out=grouped_view, in_=planes_view)
-                    else:
-                        nc.scalar.copy(out=grouped_view, in_=planes_view)
+                    nc.vector.tensor_copy(out=grouped_view, in_=planes_view)
                     codes = operand.tile([P, CHUNK], U32, name="codes", align_bytes=64)
                     scales = operand.tile([P, CHUNK], U8, name="scales", align_bytes=64)
                     nc.vector.quantize_mx(
@@ -181,16 +181,59 @@ def tile_settransform_pa_kernel(tc, set_feats, g0, b0, W0, c0, g1, b1, out):
                             start=True,
                             stop=True,
                         )
+                        if block < VECTOR_BLOCKS:
+                            nc.scalar.activation(
+                                out=h[j][:, block, :],
+                                in_=sums[:],
+                                func=FUNC.Relu,
+                                bias=bias[:, block : block + 1],
+                            )
+                            nc.vector.bn_stats(out=stats1[:, block, j, :], in_=h[j][:, block, :])
+                        else:
+                            nc.scalar.activation(
+                                out=h[j][:, block, :],
+                                in_=sums[:],
+                                func=FUNC.Relu,
+                                bias=bias[:, block : block + 1],
+                                accum_out=sum_h[:, block - VECTOR_BLOCKS, j : j + 1],
+                            )
+                    if j == 0:
+                        nc.scalar.mul(out=neg_shift[:], in_=sum_h[:, :, 0], mul=-1.0 / CHUNK)
+                    for b in range(SCALAR_BLOCKS):
+                        squares = operand.tile([P, CHUNK], F32, name="squares")
                         nc.scalar.activation(
-                            out=h[j][:, block, :],
-                            in_=sums[:],
-                            func=FUNC.Relu,
-                            bias=bias[:, block : block + 1],
+                            out=squares[:],
+                            in_=h[j][:, VECTOR_BLOCKS + b, :],
+                            func=FUNC.Square,
+                            bias=neg_shift[:, b : b + 1],
+                            accum_out=sum_sq[:, b, j : j + 1],
                         )
-                        nc.vector.bn_stats(out=stats1[:, block, j, :], in_=h[j][:, block, :])
 
+            mean_var1 = keep.tile([P, BLOCKS, 2], F32, name="mean_var1")
+            for block in range(VECTOR_BLOCKS):
+                nc.vector.bn_aggr(
+                    out=mean_var1[:, block, :],
+                    in_=stats1[:, block, :, :].rearrange("p j s -> p (j s)"),
+                )
+            scalar_mean = mean_var1[:, VECTOR_BLOCKS:, 0]
+            total_h = keep.tile([P, SCALAR_BLOCKS], F32, name="total_h")
+            nc.vector.reduce_sum(out=total_h[:], in_=sum_h[:], axis=mybir.AxisListType.X)
+            total_sq = keep.tile([P, SCALAR_BLOCKS], F32, name="total_sq")
+            nc.vector.reduce_sum(out=total_sq[:], in_=sum_sq[:], axis=mybir.AxisListType.X)
+            nc.vector.tensor_scalar_mul(out=scalar_mean, in0=total_h[:], scalar1=1.0 / ROWS)
+            gap = keep.tile([P, SCALAR_BLOCKS], F32, name="gap")
+            nc.vector.tensor_add(out=gap[:], in0=scalar_mean, in1=neg_shift[:])
+            nc.vector.tensor_mul(out=gap[:], in0=gap[:], in1=gap[:])
+            nc.vector.scalar_tensor_tensor(
+                out=mean_var1[:, VECTOR_BLOCKS:, 1],
+                in0=total_sq[:],
+                scalar=1.0 / ROWS,
+                in1=gap[:],
+                op0=ALU.mult,
+                op1=ALU.subtract,
+            )
             scale1, offset1 = norm_coefficients(
-                nc, keep, stats1, params[:, 3 * BLOCKS : 4 * BLOCKS], params[:, 4 * BLOCKS :], "norm1"
+                nc, keep, mean_var1, params[:, 3 * BLOCKS : 4 * BLOCKS], params[:, 4 * BLOCKS :], "norm1"
             )
 
             with tc.tile_pool(name="result", bufs=3) as result_pool, tc.psum_pool(

@@ -22,29 +22,37 @@ SLICES = CHUNK // P
 CHUNKS = ROWS // CHUNK
 STATS = 6
 CHUNKS_BEFORE_W = 2
-VECTOR_BLOCKS = 2
-SCALAR_BLOCKS = BLOCKS - VECTOR_BLOCKS
+VECTOR_REGROUPS_EVERY = 4
+AHEAD = 2
+STEPS = BLOCKS * CHUNKS
+DELAY = CHUNKS + 4
 
 FLOPS = 2 * ROWS * D_IN * D_OUT
 
 
-def norm_coefficients(nc, pool, mean_var, gain, shift, label):
+def norm_coefficients(nc, pool, stats, gain, shift, label):
+    n = stats.shape[1]
+    mean_var = pool.tile([P, n, 2], F32, name=label + "_mean_var")
+    for i in range(n):
+        nc.vector.bn_aggr(
+            out=mean_var[:, i, :], in_=stats[:, i, :, :].rearrange("p j s -> p (j s)")
+        )
     mean = mean_var[:, :, 0]
-    var_eps = pool.tile([P, BLOCKS], F32, name=label + "_var_eps")
+    var_eps = pool.tile([P, n], F32, name=label + "_var_eps")
     nc.vector.tensor_scalar_add(out=var_eps[:], in0=mean_var[:, :, 1], scalar1=EPS)
-    rstd = pool.tile([P, BLOCKS], F32, name=label + "_rstd")
+    rstd = pool.tile([P, n], F32, name=label + "_rstd")
     nc.scalar.sqrt(out=rstd[:], in_=var_eps[:])
     nc.vector.reciprocal(out=rstd[:], in_=rstd[:])
-    newton = pool.tile([P, BLOCKS], F32, name=label + "_newton")
+    newton = pool.tile([P, n], F32, name=label + "_newton")
     nc.vector.tensor_mul(out=newton[:], in0=rstd[:], in1=rstd[:])
     nc.vector.tensor_mul(out=newton[:], in0=newton[:], in1=var_eps[:])
     nc.vector.tensor_scalar(
         out=newton[:], in0=newton[:], scalar1=-0.5, scalar2=1.5, op0=ALU.mult, op1=ALU.add
     )
     nc.vector.tensor_mul(out=rstd[:], in0=rstd[:], in1=newton[:])
-    scale = pool.tile([P, BLOCKS], F32, name=label + "_scale")
+    scale = pool.tile([P, n], F32, name=label + "_scale")
     nc.vector.tensor_mul(out=scale[:], in0=rstd[:], in1=gain)
-    offset = pool.tile([P, BLOCKS], F32, name=label + "_offset")
+    offset = pool.tile([P, n], F32, name=label + "_offset")
     nc.vector.tensor_mul(out=offset[:], in0=mean, in1=scale[:])
     nc.vector.tensor_sub(out=offset[:], in0=shift, in1=offset[:])
     return scale, offset
@@ -68,11 +76,14 @@ def tile_settransform_pa_kernel(tc, set_feats, g0, b0, W0, c0, g1, b1, out):
         w_scales = keep.tile([P, D_OUT], U8, name="w_scales", align_bytes=64)
         params = keep.tile([P, 5 * BLOCKS], F32, name="params")
         stats0 = keep.tile([P, BLOCKS, CHUNKS, STATS], F32, name="stats0")
-        stats1 = keep.tile([P, VECTOR_BLOCKS, CHUNKS, STATS], F32, name="stats1")
-        sum_h = keep.tile([P, SCALAR_BLOCKS, CHUNKS], F32, name="sum_h")
-        sum_sq = keep.tile([P, SCALAR_BLOCKS, CHUNKS], F32, name="sum_sq")
-        neg_shift = keep.tile([P, SCALAR_BLOCKS], F32, name="neg_shift")
+        stats1 = keep.tile([P, BLOCKS, CHUNKS, STATS], F32, name="stats1")
         xt = [keep.tile([P, BLOCKS, CHUNK], BF16, name="xt%d" % j) for j in range(CHUNKS)]
+        codes = [
+            keep.tile([P, CHUNK], U32, name="codes%d" % j, align_bytes=64) for j in range(CHUNKS)
+        ]
+        scales = [
+            keep.tile([P, CHUNK], U8, name="scales%d" % j, align_bytes=64) for j in range(CHUNKS)
+        ]
 
         with tc.tile_pool(name="natural", bufs=1) as natural, tc.psum_pool(
             name="turned", bufs=6
@@ -132,136 +143,106 @@ def tile_settransform_pa_kernel(tc, set_feats, g0, b0, W0, c0, g1, b1, out):
                 for t in range(PACK):
                     nc.vector.bn_stats(out=stats0[:, t, j, :], in_=xt[j][:, t, :])
 
-        mean_var0 = keep.tile([P, BLOCKS, 2], F32, name="mean_var0")
-        for t in range(PACK):
-            nc.vector.bn_aggr(
-                out=mean_var0[:, t, :], in_=stats0[:, t, :, :].rearrange("p j s -> p (j s)")
-            )
         scale0, offset0 = norm_coefficients(
-            nc, keep, mean_var0, params[:, 0:BLOCKS], params[:, BLOCKS : 2 * BLOCKS], "norm0"
+            nc, keep, stats0, params[:, 0:BLOCKS], params[:, BLOCKS : 2 * BLOCKS], "norm0"
         )
         bias = params[:, 2 * BLOCKS : 3 * BLOCKS]
+        gain1 = params[:, 3 * BLOCKS : 4 * BLOCKS]
+        shift1 = params[:, 4 * BLOCKS : 5 * BLOCKS]
 
-        with tc.tile_pool(name="hidden", bufs=1) as hidden:
-            h = [hidden.tile([P, BLOCKS, CHUNK], F32, name="h%d" % j) for j in range(CHUNKS)]
+        with tc.tile_pool(name="grouped", bufs=3) as grouped_pool, tc.tile_pool(
+            name="hidden", bufs=DELAY + 4
+        ) as hidden_pool, tc.tile_pool(name="result", bufs=4) as result_pool, tc.psum_pool(
+            name="sums", bufs=4
+        ) as sums_pool, tc.psum_pool(name="back", bufs=4) as back_pool:
+            hidden = {}
+            norm1 = {}
 
-            with tc.tile_pool(name="operand", bufs=3) as operand, tc.psum_pool(
-                name="sums", bufs=8
-            ) as sums_pool:
-                for j in range(CHUNKS):
-                    for t in range(PACK):
-                        nc.vector.tensor_scalar(
-                            out=xt[j][:, t, :],
-                            in0=xt[j][:, t, :],
-                            scalar1=scale0[:, t : t + 1],
-                            scalar2=offset0[:, t : t + 1],
-                            op0=ALU.mult,
-                            op1=ALU.add,
-                        )
-                    grouped = operand.tile([P, CHUNK, PACK], BF16, name="grouped", align_bytes=64)
-                    grouped_view = grouped[:].rearrange("p (c i) t -> p c t i", i=4)
-                    planes_view = xt[j][:].rearrange("p t (c i) -> p c t i", i=4)
+            def prepare(j):
+                for t in range(PACK):
+                    nc.vector.tensor_scalar(
+                        out=xt[j][:, t, :],
+                        in0=xt[j][:, t, :],
+                        scalar1=scale0[:, t : t + 1],
+                        scalar2=offset0[:, t : t + 1],
+                        op0=ALU.mult,
+                        op1=ALU.add,
+                    )
+                grouped = grouped_pool.tile([P, CHUNK, PACK], BF16, name="grouped", align_bytes=64)
+                grouped_view = grouped[:].rearrange("p (c i) t -> p c t i", i=4)
+                planes_view = xt[j][:].rearrange("p t (c i) -> p c t i", i=4)
+                if j % VECTOR_REGROUPS_EVERY == 0:
                     nc.vector.tensor_copy(out=grouped_view, in_=planes_view)
-                    codes = operand.tile([P, CHUNK], U32, name="codes", align_bytes=64)
-                    scales = operand.tile([P, CHUNK], U8, name="scales", align_bytes=64)
-                    nc.vector.quantize_mx(
-                        out=codes[:].bitcast(FP8X4),
-                        scales=scales[:],
-                        in_=grouped[:].rearrange("p n t -> p (n t)"),
-                    )
-                    for block in range(BLOCKS):
-                        features = slice(block * P, (block + 1) * P)
-                        sums = sums_pool.tile([P, CHUNK], F32, name="sums")
-                        nc.tensor.matmul_mx(
-                            out=sums[:],
-                            lhsT=w_codes[:, features].bitcast(FP8X4),
-                            lhsT_scale=w_scales[:, features],
-                            rhs=codes[:].bitcast(FP8X4),
-                            rhs_scale=scales[:],
-                            start=True,
-                            stop=True,
-                        )
-                        if block < VECTOR_BLOCKS:
-                            nc.scalar.activation(
-                                out=h[j][:, block, :],
-                                in_=sums[:],
-                                func=FUNC.Relu,
-                                bias=bias[:, block : block + 1],
-                            )
-                            nc.vector.bn_stats(out=stats1[:, block, j, :], in_=h[j][:, block, :])
-                        else:
-                            nc.scalar.activation(
-                                out=h[j][:, block, :],
-                                in_=sums[:],
-                                func=FUNC.Relu,
-                                bias=bias[:, block : block + 1],
-                                accum_out=sum_h[:, block - VECTOR_BLOCKS, j : j + 1],
-                            )
-                    if j == 0:
-                        nc.scalar.mul(out=neg_shift[:], in_=sum_h[:, :, 0], mul=-1.0 / CHUNK)
-                    for b in range(SCALAR_BLOCKS):
-                        squares = operand.tile([P, CHUNK], F32, name="squares")
-                        nc.scalar.activation(
-                            out=squares[:],
-                            in_=h[j][:, VECTOR_BLOCKS + b, :],
-                            func=FUNC.Square,
-                            bias=neg_shift[:, b : b + 1],
-                            accum_out=sum_sq[:, b, j : j + 1],
-                        )
-
-            mean_var1 = keep.tile([P, BLOCKS, 2], F32, name="mean_var1")
-            for block in range(VECTOR_BLOCKS):
-                nc.vector.bn_aggr(
-                    out=mean_var1[:, block, :],
-                    in_=stats1[:, block, :, :].rearrange("p j s -> p (j s)"),
+                else:
+                    nc.scalar.copy(out=grouped_view, in_=planes_view)
+                nc.vector.quantize_mx(
+                    out=codes[j][:].bitcast(FP8X4),
+                    scales=scales[j][:],
+                    in_=grouped[:].rearrange("p n t -> p (n t)"),
                 )
-            scalar_mean = mean_var1[:, VECTOR_BLOCKS:, 0]
-            total_h = keep.tile([P, SCALAR_BLOCKS], F32, name="total_h")
-            nc.vector.reduce_sum(out=total_h[:], in_=sum_h[:], axis=mybir.AxisListType.X)
-            total_sq = keep.tile([P, SCALAR_BLOCKS], F32, name="total_sq")
-            nc.vector.reduce_sum(out=total_sq[:], in_=sum_sq[:], axis=mybir.AxisListType.X)
-            nc.vector.tensor_scalar_mul(out=scalar_mean, in0=total_h[:], scalar1=1.0 / ROWS)
-            gap = keep.tile([P, SCALAR_BLOCKS], F32, name="gap")
-            nc.vector.tensor_add(out=gap[:], in0=scalar_mean, in1=neg_shift[:])
-            nc.vector.tensor_mul(out=gap[:], in0=gap[:], in1=gap[:])
-            nc.vector.scalar_tensor_tensor(
-                out=mean_var1[:, VECTOR_BLOCKS:, 1],
-                in0=total_sq[:],
-                scalar=1.0 / ROWS,
-                in1=gap[:],
-                op0=ALU.mult,
-                op1=ALU.subtract,
-            )
-            scale1, offset1 = norm_coefficients(
-                nc, keep, mean_var1, params[:, 3 * BLOCKS : 4 * BLOCKS], params[:, 4 * BLOCKS :], "norm1"
-            )
 
-            with tc.tile_pool(name="result", bufs=3) as result_pool, tc.psum_pool(
-                name="back", bufs=8
-            ) as back_pool:
-                for j in range(CHUNKS):
-                    for block in range(BLOCKS):
-                        nc.vector.tensor_scalar(
-                            out=h[j][:, block, :],
-                            in0=h[j][:, block, :],
-                            scalar1=scale1[:, block : block + 1],
-                            scalar2=offset1[:, block : block + 1],
-                            op0=ALU.mult,
-                            op1=ALU.add,
-                        )
-                    result = result_pool.tile([P, SLICES, D_OUT], F32, name="result")
-                    for s in range(SLICES):
-                        back = back_pool.tile([P, D_OUT], F32, name="back")
-                        for block in range(BLOCKS):
-                            nc.tensor.transpose(
-                                out=back[:, block * P : (block + 1) * P],
-                                in_=h[j][:, block, s * P : (s + 1) * P],
-                                identity=ident_f32[:],
-                            )
-                        if s == SLICES - 1:
-                            nc.vector.tensor_copy(out=result[:, s, :], in_=back[:])
-                        else:
-                            nc.scalar.copy(out=result[:, s, :], in_=back[:])
-                    nc.sync.dma_start(
-                        out=out_rows[:, j * SLICES : (j + 1) * SLICES, :], in_=result[:]
+            def multiply(block, j):
+                features = slice(block * P, (block + 1) * P)
+                sums = sums_pool.tile([P, CHUNK], F32, name="sums")
+                nc.tensor.matmul_mx(
+                    out=sums[:],
+                    lhsT=w_codes[:, features].bitcast(FP8X4),
+                    lhsT_scale=w_scales[:, features],
+                    rhs=codes[j][:].bitcast(FP8X4),
+                    rhs_scale=scales[j][:],
+                    start=True,
+                    stop=True,
+                )
+                h = hidden_pool.tile([P, CHUNK], F32, name="h")
+                nc.scalar.activation(
+                    out=h[:], in_=sums[:], func=FUNC.Relu, bias=bias[:, block : block + 1]
+                )
+                nc.vector.bn_stats(out=stats1[:, block, j, :], in_=h[:])
+                hidden[(block, j)] = h
+
+            def finish(block, j):
+                h = hidden[(block, j)]
+                scale1, offset1 = norm1[block]
+                norm_engine = nc.vector if block == BLOCKS - 1 else nc.gpsimd
+                norm_engine.tensor_scalar(
+                    out=h[:],
+                    in0=h[:],
+                    scalar1=scale1[:],
+                    scalar2=offset1[:],
+                    op0=ALU.mult,
+                    op1=ALU.add,
+                )
+                back = back_pool.tile([P, SLICES, P], F32, name="back")
+                for s in range(SLICES):
+                    nc.tensor.transpose(
+                        out=back[:, s, :], in_=h[:, s * P : (s + 1) * P], identity=ident_f32[:]
                     )
+                result = result_pool.tile([P, SLICES, P], F32, name="result")
+                if j % 2 == 0:
+                    nc.scalar.copy(out=result[:], in_=back[:])
+                else:
+                    nc.vector.tensor_copy(out=result[:], in_=back[:])
+                nc.sync.dma_start(
+                    out=out_rows[:, j * SLICES : (j + 1) * SLICES, block * P : (block + 1) * P],
+                    in_=result[:],
+                )
+
+            for j in range(AHEAD):
+                prepare(j)
+            for step in range(STEPS + DELAY):
+                if step + AHEAD < CHUNKS:
+                    prepare(step + AHEAD)
+                if step < STEPS:
+                    block = step // CHUNKS
+                    multiply(block, step % CHUNKS)
+                    if step % CHUNKS == CHUNKS - 1:
+                        norm1[block] = norm_coefficients(
+                            nc,
+                            keep,
+                            stats1[:, block : block + 1, :, :],
+                            gain1[:, block : block + 1],
+                            shift1[:, block : block + 1],
+                            "norm1_%d" % block,
+                        )
+                if step >= DELAY:
+                    finish((step - DELAY) // CHUNKS, (step - DELAY) % CHUNKS)

@@ -8,6 +8,7 @@ U8 = mybir.dt.uint8
 FP8X4 = mybir.dt.float8_e4m3fn_x4
 ALU = mybir.AluOpType
 FUNC = mybir.ActivationFunctionType
+AXIS = mybir.AxisListType
 
 P = 128
 PACK = 4
@@ -22,37 +23,58 @@ SLICES = CHUNK // P
 CHUNKS = ROWS // CHUNK
 STATS = 6
 CHUNKS_BEFORE_W = 2
-VECTOR_REGROUPS_EVERY = 4
-AHEAD = 2
-STEPS = BLOCKS * CHUNKS
-DELAY = CHUNKS + 4
+VECTOR_IN = 3
+SCALAR_IN = BLOCKS - VECTOR_IN
+VECTOR_OUT = 2
+SCALAR_OUT = BLOCKS - VECTOR_OUT
+ONES = 32
 
 FLOPS = 2 * ROWS * D_IN * D_OUT
 
 
-def norm_coefficients(nc, pool, stats, gain, shift, label):
-    n = stats.shape[1]
-    mean_var = pool.tile([P, n, 2], F32, name=label + "_mean_var")
-    for i in range(n):
+def mean_var_from_records(nc, mean_var, stats):
+    for i in range(stats.shape[1]):
         nc.vector.bn_aggr(
             out=mean_var[:, i, :], in_=stats[:, i, :, :].rearrange("p j s -> p (j s)")
         )
+
+
+def mean_var_from_sums(nc, pool, mean_var, total, squares, shift, label):
+    n = total.shape[1]
     mean = mean_var[:, :, 0]
-    var_eps = pool.tile([P, n], F32, name=label + "_var_eps")
+    nc.vector.tensor_scalar_mul(out=mean, in0=total, scalar1=1.0 / ROWS)
+    gap = pool.tile([P, n], F32, name=label + "_gap")
+    nc.vector.tensor_sub(out=gap[:], in0=mean, in1=shift)
+    nc.vector.tensor_mul(out=gap[:], in0=gap[:], in1=gap[:])
+    total_sq = pool.tile([P, n], F32, name=label + "_total_sq")
+    nc.vector.reduce_sum(out=total_sq[:], in_=squares, axis=AXIS.X)
+    nc.vector.scalar_tensor_tensor(
+        out=mean_var[:, :, 1],
+        in0=total_sq[:],
+        scalar=1.0 / ROWS,
+        in1=gap[:],
+        op0=ALU.mult,
+        op1=ALU.subtract,
+    )
+
+
+def norm_coefficients(nc, pool, mean_var, gain, shift, label):
+    mean = mean_var[:, :, 0]
+    var_eps = pool.tile([P, BLOCKS], F32, name=label + "_var_eps")
     nc.vector.tensor_scalar_add(out=var_eps[:], in0=mean_var[:, :, 1], scalar1=EPS)
-    rstd = pool.tile([P, n], F32, name=label + "_rstd")
+    rstd = pool.tile([P, BLOCKS], F32, name=label + "_rstd")
     nc.scalar.sqrt(out=rstd[:], in_=var_eps[:])
     nc.vector.reciprocal(out=rstd[:], in_=rstd[:])
-    newton = pool.tile([P, n], F32, name=label + "_newton")
+    newton = pool.tile([P, BLOCKS], F32, name=label + "_newton")
     nc.vector.tensor_mul(out=newton[:], in0=rstd[:], in1=rstd[:])
     nc.vector.tensor_mul(out=newton[:], in0=newton[:], in1=var_eps[:])
     nc.vector.tensor_scalar(
         out=newton[:], in0=newton[:], scalar1=-0.5, scalar2=1.5, op0=ALU.mult, op1=ALU.add
     )
     nc.vector.tensor_mul(out=rstd[:], in0=rstd[:], in1=newton[:])
-    scale = pool.tile([P, n], F32, name=label + "_scale")
+    scale = pool.tile([P, BLOCKS], F32, name=label + "_scale")
     nc.vector.tensor_mul(out=scale[:], in0=rstd[:], in1=gain)
-    offset = pool.tile([P, n], F32, name=label + "_offset")
+    offset = pool.tile([P, BLOCKS], F32, name=label + "_offset")
     nc.vector.tensor_mul(out=offset[:], in0=mean, in1=scale[:])
     nc.vector.tensor_sub(out=offset[:], in0=shift, in1=offset[:])
     return scale, offset
@@ -63,11 +85,13 @@ def tile_settransform_pa_kernel(tc, set_feats, g0, b0, W0, c0, g1, b1, out):
     x_rows = set_feats.flatten_outer_dims().rearrange("(p c) k -> p c k", c=ROWS_PER_PARTITION)
     out_rows = out.flatten_outer_dims().rearrange("(p c) f -> p c f", c=ROWS_PER_PARTITION)
 
-    with tc.tile_pool(name="keep", bufs=1) as keep:
+    with tc.tile_pool(name="keep", bufs=1) as keep, tc.tile_pool(name="waste", bufs=2) as waste:
         ident_bf16 = keep.tile([P, P], BF16, name="ident_bf16")
         make_identity(nc, ident_bf16[:])
         ident_f32 = keep.tile([P, P], F32, name="ident_f32")
         make_identity(nc, ident_f32[:])
+        ones = keep.tile([P, ONES], BF16, name="ones")
+        nc.vector.memset(ones[:], 1.0)
         warm = keep.tile([P, 1], F32, name="warm")
         nc.vector.memset(warm[:], 1.0)
         nc.scalar.sqrt(out=warm[:], in_=warm[:])
@@ -75,19 +99,27 @@ def tile_settransform_pa_kernel(tc, set_feats, g0, b0, W0, c0, g1, b1, out):
         w_codes = keep.tile([P, D_OUT], U32, name="w_codes", align_bytes=64)
         w_scales = keep.tile([P, D_OUT], U8, name="w_scales", align_bytes=64)
         params = keep.tile([P, 5 * BLOCKS], F32, name="params")
-        stats0 = keep.tile([P, BLOCKS, CHUNKS, STATS], F32, name="stats0")
-        stats1 = keep.tile([P, BLOCKS, CHUNKS, STATS], F32, name="stats1")
         xt = [keep.tile([P, BLOCKS, CHUNK], BF16, name="xt%d" % j) for j in range(CHUNKS)]
-        codes = [
-            keep.tile([P, CHUNK], U32, name="codes%d" % j, align_bytes=64) for j in range(CHUNKS)
-        ]
-        scales = [
-            keep.tile([P, CHUNK], U8, name="scales%d" % j, align_bytes=64) for j in range(CHUNKS)
-        ]
 
+        def sum_of_squares(values, shift, accum_out):
+            squares = waste.tile([P, CHUNK], F32, name="squares")
+            nc.scalar.activation(
+                out=squares[:],
+                in_=values,
+                func=FUNC.Square,
+                scale=-1.0,
+                bias=shift,
+                accum_out=accum_out,
+            )
+
+        stats_in = keep.tile([P, VECTOR_IN, CHUNKS, STATS], F32, name="stats_in")
+        squares_in = keep.tile([P, SCALAR_IN, CHUNKS], F32, name="squares_in")
+        first_in = keep.tile([P, SCALAR_IN, STATS], F32, name="first_in")
+        shift_in = first_in[:, :, 1]
+        mean_var_in = keep.tile([P, BLOCKS, 2], F32, name="mean_var_in")
         with tc.tile_pool(name="natural", bufs=1) as natural, tc.psum_pool(
             name="turned", bufs=6
-        ) as turned_pool:
+        ) as turned_pool, tc.psum_pool(name="total", bufs=1) as total_pool:
             x_nat = [natural.tile([P, SLICES, D_IN], BF16, name="x_nat%d" % j) for j in range(CHUNKS)]
             w_nat = natural.tile([P, BLOCKS, D_IN], BF16, name="w_nat")
             for j in range(CHUNKS):
@@ -104,6 +136,7 @@ def tile_settransform_pa_kernel(tc, set_feats, g0, b0, W0, c0, g1, b1, out):
                     in_=vec.rearrange("(t p) -> t p", p=P),
                 )
 
+            total_in = total_pool.tile([P, SCALAR_IN, ONES], F32, name="total_in")
             for j in range(CHUNKS):
                 if j == CHUNKS_BEFORE_W:
                     w_grouped = natural.tile(
@@ -140,109 +173,154 @@ def tile_settransform_pa_kernel(tc, set_feats, g0, b0, W0, c0, g1, b1, out):
                             identity=ident_bf16[:],
                         )
                     nc.scalar.copy(out=xt[j][:, :, s * P : (s + 1) * P], in_=x_turned[:])
-                for t in range(PACK):
-                    nc.vector.bn_stats(out=stats0[:, t, j, :], in_=xt[j][:, t, :])
+                    for i in range(SCALAR_IN):
+                        t = VECTOR_IN + i
+                        nc.tensor.matmul(
+                            out=total_in[:, i, :],
+                            lhsT=x_nat[j][:, s, t * P : (t + 1) * P],
+                            rhs=ones[:],
+                            start=(j == 0 and s == 0),
+                            stop=(j == CHUNKS - 1 and s == SLICES - 1),
+                        )
+                for t in range(VECTOR_IN):
+                    nc.vector.bn_stats(out=stats_in[:, t, j, :], in_=xt[j][:, t, :])
+                for i in range(SCALAR_IN):
+                    if j == 0:
+                        nc.vector.bn_stats(out=first_in[:, i, :], in_=xt[j][:, VECTOR_IN + i, :])
+                    sum_of_squares(
+                        xt[j][:, VECTOR_IN + i, :],
+                        shift_in[:, i : i + 1],
+                        squares_in[:, i, j : j + 1],
+                    )
 
-        scale0, offset0 = norm_coefficients(
-            nc, keep, stats0, params[:, 0:BLOCKS], params[:, BLOCKS : 2 * BLOCKS], "norm0"
+            mean_var_from_records(nc, mean_var_in[:, 0:VECTOR_IN, :], stats_in)
+            mean_var_from_sums(
+                nc,
+                keep,
+                mean_var_in[:, VECTOR_IN:, :],
+                total_in[:, :, 0],
+                squares_in[:],
+                shift_in,
+                "in",
+            )
+
+        scale_in, offset_in = norm_coefficients(
+            nc, keep, mean_var_in, params[:, 0:BLOCKS], params[:, BLOCKS : 2 * BLOCKS], "in"
         )
         bias = params[:, 2 * BLOCKS : 3 * BLOCKS]
-        gain1 = params[:, 3 * BLOCKS : 4 * BLOCKS]
-        shift1 = params[:, 4 * BLOCKS : 5 * BLOCKS]
 
-        with tc.tile_pool(name="grouped", bufs=3) as grouped_pool, tc.tile_pool(
-            name="hidden", bufs=DELAY + 4
-        ) as hidden_pool, tc.tile_pool(name="result", bufs=4) as result_pool, tc.psum_pool(
-            name="sums", bufs=4
-        ) as sums_pool, tc.psum_pool(name="back", bufs=4) as back_pool:
-            hidden = {}
-            norm1 = {}
+        stats_out = keep.tile([P, VECTOR_OUT, CHUNKS, STATS], F32, name="stats_out")
+        sums_out = keep.tile([P, SCALAR_OUT, CHUNKS], F32, name="sums_out")
+        squares_out = keep.tile([P, SCALAR_OUT, CHUNKS], F32, name="squares_out")
+        shift_out = keep.tile([P, SCALAR_OUT], F32, name="shift_out")
+        mean_var_out = keep.tile([P, BLOCKS, 2], F32, name="mean_var_out")
+        with tc.tile_pool(name="hidden", bufs=1) as hidden:
+            h = [hidden.tile([P, BLOCKS, CHUNK], F32, name="h%d" % j) for j in range(CHUNKS)]
 
-            def prepare(j):
-                for t in range(PACK):
-                    nc.vector.tensor_scalar(
-                        out=xt[j][:, t, :],
-                        in0=xt[j][:, t, :],
-                        scalar1=scale0[:, t : t + 1],
-                        scalar2=offset0[:, t : t + 1],
-                        op0=ALU.mult,
-                        op1=ALU.add,
-                    )
-                grouped = grouped_pool.tile([P, CHUNK, PACK], BF16, name="grouped", align_bytes=64)
-                grouped_view = grouped[:].rearrange("p (c i) t -> p c t i", i=4)
-                planes_view = xt[j][:].rearrange("p t (c i) -> p c t i", i=4)
-                if j % VECTOR_REGROUPS_EVERY == 0:
-                    nc.vector.tensor_copy(out=grouped_view, in_=planes_view)
-                else:
-                    nc.scalar.copy(out=grouped_view, in_=planes_view)
-                nc.vector.quantize_mx(
-                    out=codes[j][:].bitcast(FP8X4),
-                    scales=scales[j][:],
-                    in_=grouped[:].rearrange("p n t -> p (n t)"),
-                )
-
-            def multiply(block, j):
-                features = slice(block * P, (block + 1) * P)
-                sums = sums_pool.tile([P, CHUNK], F32, name="sums")
-                nc.tensor.matmul_mx(
-                    out=sums[:],
-                    lhsT=w_codes[:, features].bitcast(FP8X4),
-                    lhsT_scale=w_scales[:, features],
-                    rhs=codes[j][:].bitcast(FP8X4),
-                    rhs_scale=scales[j][:],
-                    start=True,
-                    stop=True,
-                )
-                h = hidden_pool.tile([P, CHUNK], F32, name="h")
-                nc.scalar.activation(
-                    out=h[:], in_=sums[:], func=FUNC.Relu, bias=bias[:, block : block + 1]
-                )
-                nc.vector.bn_stats(out=stats1[:, block, j, :], in_=h[:])
-                hidden[(block, j)] = h
-
-            def finish(block, j):
-                h = hidden[(block, j)]
-                scale1, offset1 = norm1[block]
-                norm_engine = nc.vector if block == BLOCKS - 1 else nc.gpsimd
-                norm_engine.tensor_scalar(
-                    out=h[:],
-                    in0=h[:],
-                    scalar1=scale1[:],
-                    scalar2=offset1[:],
-                    op0=ALU.mult,
-                    op1=ALU.add,
-                )
-                back = back_pool.tile([P, SLICES, P], F32, name="back")
-                for s in range(SLICES):
-                    nc.tensor.transpose(
-                        out=back[:, s, :], in_=h[:, s * P : (s + 1) * P], identity=ident_f32[:]
-                    )
-                result = result_pool.tile([P, SLICES, P], F32, name="result")
-                if j % 2 == 0:
-                    nc.scalar.copy(out=result[:], in_=back[:])
-                else:
-                    nc.vector.tensor_copy(out=result[:], in_=back[:])
-                nc.sync.dma_start(
-                    out=out_rows[:, j * SLICES : (j + 1) * SLICES, block * P : (block + 1) * P],
-                    in_=result[:],
-                )
-
-            for j in range(AHEAD):
-                prepare(j)
-            for step in range(STEPS + DELAY):
-                if step + AHEAD < CHUNKS:
-                    prepare(step + AHEAD)
-                if step < STEPS:
-                    block = step // CHUNKS
-                    multiply(block, step % CHUNKS)
-                    if step % CHUNKS == CHUNKS - 1:
-                        norm1[block] = norm_coefficients(
-                            nc,
-                            keep,
-                            stats1[:, block : block + 1, :, :],
-                            gain1[:, block : block + 1],
-                            shift1[:, block : block + 1],
-                            "norm1_%d" % block,
+            with tc.tile_pool(name="operand", bufs=3) as operand, tc.psum_pool(
+                name="sums", bufs=8
+            ) as sums_pool:
+                for j in range(CHUNKS):
+                    for t in range(PACK):
+                        nc.vector.tensor_scalar(
+                            out=xt[j][:, t, :],
+                            in0=xt[j][:, t, :],
+                            scalar1=scale_in[:, t : t + 1],
+                            scalar2=offset_in[:, t : t + 1],
+                            op0=ALU.mult,
+                            op1=ALU.add,
                         )
-                if step >= DELAY:
-                    finish((step - DELAY) // CHUNKS, (step - DELAY) % CHUNKS)
+                    grouped = operand.tile([P, CHUNK, PACK], BF16, name="grouped", align_bytes=64)
+                    nc.vector.tensor_copy(
+                        out=grouped[:].rearrange("p (c i) t -> p c t i", i=4),
+                        in_=xt[j][:].rearrange("p t (c i) -> p c t i", i=4),
+                    )
+                    codes = operand.tile([P, CHUNK], U32, name="codes", align_bytes=64)
+                    scales = operand.tile([P, CHUNK], U8, name="scales", align_bytes=64)
+                    nc.vector.quantize_mx(
+                        out=codes[:].bitcast(FP8X4),
+                        scales=scales[:],
+                        in_=grouped[:].rearrange("p n t -> p (n t)"),
+                    )
+                    for block in range(BLOCKS):
+                        features = slice(block * P, (block + 1) * P)
+                        sums = sums_pool.tile([P, CHUNK], F32, name="sums")
+                        nc.tensor.matmul_mx(
+                            out=sums[:],
+                            lhsT=w_codes[:, features].bitcast(FP8X4),
+                            lhsT_scale=w_scales[:, features],
+                            rhs=codes[:].bitcast(FP8X4),
+                            rhs_scale=scales[:],
+                            start=True,
+                            stop=True,
+                        )
+                        if block < VECTOR_OUT:
+                            nc.scalar.activation(
+                                out=h[j][:, block, :],
+                                in_=sums[:],
+                                func=FUNC.Relu,
+                                bias=bias[:, block : block + 1],
+                            )
+                            nc.vector.bn_stats(out=stats_out[:, block, j, :], in_=h[j][:, block, :])
+                        else:
+                            nc.scalar.activation(
+                                out=h[j][:, block, :],
+                                in_=sums[:],
+                                func=FUNC.Relu,
+                                bias=bias[:, block : block + 1],
+                                accum_out=sums_out[:, block - VECTOR_OUT, j : j + 1],
+                            )
+                    if j == 0:
+                        nc.scalar.mul(out=shift_out[:], in_=sums_out[:, :, 0], mul=1.0 / CHUNK)
+                    for i in range(SCALAR_OUT):
+                        sum_of_squares(
+                            h[j][:, VECTOR_OUT + i, :],
+                            shift_out[:, i : i + 1],
+                            squares_out[:, i, j : j + 1],
+                        )
+
+            mean_var_from_records(nc, mean_var_out[:, 0:VECTOR_OUT, :], stats_out)
+            total_out = keep.tile([P, SCALAR_OUT], F32, name="total_out")
+            nc.vector.reduce_sum(out=total_out[:], in_=sums_out[:], axis=AXIS.X)
+            mean_var_from_sums(
+                nc,
+                keep,
+                mean_var_out[:, VECTOR_OUT:, :],
+                total_out[:],
+                squares_out[:],
+                shift_out[:],
+                "out",
+            )
+            scale_out, offset_out = norm_coefficients(
+                nc, keep, mean_var_out, params[:, 3 * BLOCKS : 4 * BLOCKS], params[:, 4 * BLOCKS :], "out"
+            )
+
+            with tc.tile_pool(name="result", bufs=3) as result_pool, tc.psum_pool(
+                name="back", bufs=8
+            ) as back_pool:
+                for j in range(CHUNKS):
+                    for block in range(BLOCKS):
+                        nc.vector.tensor_scalar(
+                            out=h[j][:, block, :],
+                            in0=h[j][:, block, :],
+                            scalar1=scale_out[:, block : block + 1],
+                            scalar2=offset_out[:, block : block + 1],
+                            op0=ALU.mult,
+                            op1=ALU.add,
+                        )
+                    result = result_pool.tile([P, SLICES, D_OUT], F32, name="result")
+                    for s in range(SLICES):
+                        back = back_pool.tile([P, D_OUT], F32, name="back")
+                        for block in range(BLOCKS):
+                            nc.tensor.transpose(
+                                out=back[:, block * P : (block + 1) * P],
+                                in_=h[j][:, block, s * P : (s + 1) * P],
+                                identity=ident_f32[:],
+                            )
+                        if s == SLICES - 1:
+                            nc.vector.tensor_copy(out=result[:, s, :], in_=back[:])
+                        else:
+                            nc.scalar.copy(out=result[:, s, :], in_=back[:])
+                    nc.sync.dma_start(
+                        out=out_rows[:, j * SLICES : (j + 1) * SLICES, :], in_=result[:]
+                    )

import concourse.mybir as mybir
from concourse.masks import make_identity

F32 = mybir.dt.float32
BF16 = mybir.dt.bfloat16
U32 = mybir.dt.uint32
U8 = mybir.dt.uint8
FP8X4 = mybir.dt.float8_e4m3fn_x4
ALU = mybir.AluOpType
FUNC = mybir.ActivationFunctionType
AXIS = mybir.AxisListType

P = 128
PACK = 4
ROWS = 64 * 128
D_IN = 512
D_OUT = 512
EPS = 1e-5
BLOCKS = 4
ROWS_PER_PARTITION = ROWS // P
CHUNK = 512
SLICES = CHUNK // P
CHUNKS = ROWS // CHUNK
STATS = 6
CHUNKS_BEFORE_W = 2
VECTOR_IN = 3
SCALAR_IN = BLOCKS - VECTOR_IN
VECTOR_OUT = 2
SCALAR_OUT = BLOCKS - VECTOR_OUT
ONES = 32

FLOPS = 2 * ROWS * D_IN * D_OUT


def mean_var_from_records(nc, mean_var, stats):
    for i in range(stats.shape[1]):
        nc.vector.bn_aggr(
            out=mean_var[:, i, :], in_=stats[:, i, :, :].rearrange("p j s -> p (j s)")
        )


def mean_var_from_sums(nc, pool, mean_var, total, squares, shift, label):
    n = total.shape[1]
    mean = mean_var[:, :, 0]
    nc.vector.tensor_scalar_mul(out=mean, in0=total, scalar1=1.0 / ROWS)
    gap = pool.tile([P, n], F32, name=label + "_gap")
    nc.vector.tensor_sub(out=gap[:], in0=mean, in1=shift)
    nc.vector.tensor_mul(out=gap[:], in0=gap[:], in1=gap[:])
    total_sq = pool.tile([P, n], F32, name=label + "_total_sq")
    nc.vector.reduce_sum(out=total_sq[:], in_=squares, axis=AXIS.X)
    nc.vector.scalar_tensor_tensor(
        out=mean_var[:, :, 1],
        in0=total_sq[:],
        scalar=1.0 / ROWS,
        in1=gap[:],
        op0=ALU.mult,
        op1=ALU.subtract,
    )


def norm_coefficients(nc, pool, mean_var, gain, shift, label):
    mean = mean_var[:, :, 0]
    var_eps = pool.tile([P, BLOCKS], F32, name=label + "_var_eps")
    nc.vector.tensor_scalar_add(out=var_eps[:], in0=mean_var[:, :, 1], scalar1=EPS)
    rstd = pool.tile([P, BLOCKS], F32, name=label + "_rstd")
    nc.scalar.sqrt(out=rstd[:], in_=var_eps[:])
    nc.vector.reciprocal(out=rstd[:], in_=rstd[:])
    newton = pool.tile([P, BLOCKS], F32, name=label + "_newton")
    nc.vector.tensor_mul(out=newton[:], in0=rstd[:], in1=rstd[:])
    nc.vector.tensor_mul(out=newton[:], in0=newton[:], in1=var_eps[:])
    nc.vector.tensor_scalar(
        out=newton[:], in0=newton[:], scalar1=-0.5, scalar2=1.5, op0=ALU.mult, op1=ALU.add
    )
    nc.vector.tensor_mul(out=rstd[:], in0=rstd[:], in1=newton[:])
    scale = pool.tile([P, BLOCKS], F32, name=label + "_scale")
    nc.vector.tensor_mul(out=scale[:], in0=rstd[:], in1=gain)
    offset = pool.tile([P, BLOCKS], F32, name=label + "_offset")
    nc.vector.tensor_mul(out=offset[:], in0=mean, in1=scale[:])
    nc.vector.tensor_sub(out=offset[:], in0=shift, in1=offset[:])
    return scale, offset


def tile_settransform_pa_kernel(tc, set_feats, g0, b0, W0, c0, g1, b1, out):
    nc = tc.nc
    x_rows = set_feats.flatten_outer_dims().rearrange("(p c) k -> p c k", c=ROWS_PER_PARTITION)
    out_rows = out.flatten_outer_dims().rearrange("(p c) f -> p c f", c=ROWS_PER_PARTITION)

    with tc.tile_pool(name="keep", bufs=1) as keep, tc.tile_pool(name="waste", bufs=2) as waste:
        ident_bf16 = keep.tile([P, P], BF16, name="ident_bf16")
        make_identity(nc, ident_bf16[:])
        ident_f32 = keep.tile([P, P], F32, name="ident_f32")
        make_identity(nc, ident_f32[:])
        ones = keep.tile([P, ONES], BF16, name="ones")
        nc.vector.memset(ones[:], 1.0)
        warm = keep.tile([P, 1], F32, name="warm")
        nc.vector.memset(warm[:], 1.0)
        nc.scalar.sqrt(out=warm[:], in_=warm[:])

        w_codes = keep.tile([P, D_OUT], U32, name="w_codes", align_bytes=64)
        w_scales = keep.tile([P, D_OUT], U8, name="w_scales", align_bytes=64)
        params = keep.tile([P, 5 * BLOCKS], F32, name="params")
        xt = [keep.tile([P, BLOCKS, CHUNK], BF16, name="xt%d" % j) for j in range(CHUNKS)]

        def sum_of_squares(values, shift, accum_out):
            squares = waste.tile([P, CHUNK], F32, name="squares")
            nc.scalar.activation(
                out=squares[:],
                in_=values,
                func=FUNC.Square,
                scale=-1.0,
                bias=shift,
                accum_out=accum_out,
            )

        stats_in = keep.tile([P, VECTOR_IN, CHUNKS, STATS], F32, name="stats_in")
        squares_in = keep.tile([P, SCALAR_IN, CHUNKS], F32, name="squares_in")
        first_in = keep.tile([P, SCALAR_IN, STATS], F32, name="first_in")
        shift_in = first_in[:, :, 1]
        mean_var_in = keep.tile([P, BLOCKS, 2], F32, name="mean_var_in")
        with tc.tile_pool(name="natural", bufs=1) as natural, tc.psum_pool(
            name="turned", bufs=6
        ) as turned_pool, tc.psum_pool(name="total", bufs=1) as total_pool:
            x_nat = [natural.tile([P, SLICES, D_IN], BF16, name="x_nat%d" % j) for j in range(CHUNKS)]
            w_nat = natural.tile([P, BLOCKS, D_IN], BF16, name="w_nat")
            for j in range(CHUNKS):
                if j == CHUNKS_BEFORE_W:
                    nc.sync.dma_start(out=w_nat[:], in_=W0.rearrange("(b f) k -> f b k", f=P))
                nc.sync.dma_start(
                    out=x_nat[j][:], in_=x_rows[:, j * SLICES : (j + 1) * SLICES, :]
                )
            vec_rows = natural.tile([P, P], BF16, name="vec_rows")
            nc.vector.memset(vec_rows[:], 0.0)
            for v, vec in enumerate((g0, b0, c0, g1, b1)):
                nc.scalar.dma_start(
                    out=vec_rows[BLOCKS * v : BLOCKS * (v + 1), :],
                    in_=vec.rearrange("(t p) -> t p", p=P),
                )

            total_in = total_pool.tile([P, SCALAR_IN, ONES], F32, name="total_in")
            for j in range(CHUNKS):
                if j == CHUNKS_BEFORE_W:
                    w_grouped = natural.tile(
                        [P, D_OUT, PACK], BF16, name="w_grouped", align_bytes=64
                    )
                    for block in range(BLOCKS):
                        w_turned = turned_pool.tile([P, PACK, P], BF16, tag="turned")
                        for t in range(PACK):
                            nc.tensor.transpose(
                                out=w_turned[:, t, :],
                                in_=w_nat[:, block, t * P : (t + 1) * P],
                                identity=ident_bf16[:],
                            )
                        nc.scalar.copy(
                            out=w_grouped[:, block * P : (block + 1) * P, :],
                            in_=w_turned[:].rearrange("p t f -> p f t"),
                        )
                    nc.vector.quantize_mx(
                        out=w_codes[:].bitcast(FP8X4),
                        scales=w_scales[:],
                        in_=w_grouped[:].rearrange("p f t -> p (f t)"),
                    )
                    vec_turned = turned_pool.tile([P, PACK, P], BF16, tag="turned")
                    nc.tensor.transpose(
                        out=vec_turned[:, 0, :], in_=vec_rows[:], identity=ident_bf16[:]
                    )
                    nc.vector.tensor_copy(out=params[:], in_=vec_turned[:, 0, 0 : 5 * BLOCKS])
                for s in range(SLICES):
                    x_turned = turned_pool.tile([P, PACK, P], BF16, tag="turned")
                    for t in range(PACK):
                        nc.tensor.transpose(
                            out=x_turned[:, t, :],
                            in_=x_nat[j][:, s, t * P : (t + 1) * P],
                            identity=ident_bf16[:],
                        )
                    nc.scalar.copy(out=xt[j][:, :, s * P : (s + 1) * P], in_=x_turned[:])
                    for i in range(SCALAR_IN):
                        t = VECTOR_IN + i
                        nc.tensor.matmul(
                            out=total_in[:, i, :],
                            lhsT=x_nat[j][:, s, t * P : (t + 1) * P],
                            rhs=ones[:],
                            start=(j == 0 and s == 0),
                            stop=(j == CHUNKS - 1 and s == SLICES - 1),
                        )
                for t in range(VECTOR_IN):
                    nc.vector.bn_stats(out=stats_in[:, t, j, :], in_=xt[j][:, t, :])
                for i in range(SCALAR_IN):
                    if j == 0:
                        nc.vector.bn_stats(out=first_in[:, i, :], in_=xt[j][:, VECTOR_IN + i, :])
                    sum_of_squares(
                        xt[j][:, VECTOR_IN + i, :],
                        shift_in[:, i : i + 1],
                        squares_in[:, i, j : j + 1],
                    )

            mean_var_from_records(nc, mean_var_in[:, 0:VECTOR_IN, :], stats_in)
            mean_var_from_sums(
                nc,
                keep,
                mean_var_in[:, VECTOR_IN:, :],
                total_in[:, :, 0],
                squares_in[:],
                shift_in,
                "in",
            )

        scale_in, offset_in = norm_coefficients(
            nc, keep, mean_var_in, params[:, 0:BLOCKS], params[:, BLOCKS : 2 * BLOCKS], "in"
        )
        bias = params[:, 2 * BLOCKS : 3 * BLOCKS]

        stats_out = keep.tile([P, VECTOR_OUT, CHUNKS, STATS], F32, name="stats_out")
        sums_out = keep.tile([P, SCALAR_OUT, CHUNKS], F32, name="sums_out")
        squares_out = keep.tile([P, SCALAR_OUT, CHUNKS], F32, name="squares_out")
        shift_out = keep.tile([P, SCALAR_OUT], F32, name="shift_out")
        mean_var_out = keep.tile([P, BLOCKS, 2], F32, name="mean_var_out")
        with tc.tile_pool(name="hidden", bufs=1) as hidden:
            h = [hidden.tile([P, BLOCKS, CHUNK], F32, name="h%d" % j) for j in range(CHUNKS)]

            with tc.tile_pool(name="operand", bufs=3) as operand, tc.psum_pool(
                name="sums", bufs=8
            ) as sums_pool:
                for j in range(CHUNKS):
                    for t in range(PACK):
                        nc.vector.tensor_scalar(
                            out=xt[j][:, t, :],
                            in0=xt[j][:, t, :],
                            scalar1=scale_in[:, t : t + 1],
                            scalar2=offset_in[:, t : t + 1],
                            op0=ALU.mult,
                            op1=ALU.add,
                        )
                    grouped = operand.tile([P, CHUNK, PACK], BF16, name="grouped", align_bytes=64)
                    nc.vector.tensor_copy(
                        out=grouped[:].rearrange("p (c i) t -> p c t i", i=4),
                        in_=xt[j][:].rearrange("p t (c i) -> p c t i", i=4),
                    )
                    codes = operand.tile([P, CHUNK], U32, name="codes", align_bytes=64)
                    scales = operand.tile([P, CHUNK], U8, name="scales", align_bytes=64)
                    nc.vector.quantize_mx(
                        out=codes[:].bitcast(FP8X4),
                        scales=scales[:],
                        in_=grouped[:].rearrange("p n t -> p (n t)"),
                    )
                    for block in range(BLOCKS):
                        features = slice(block * P, (block + 1) * P)
                        sums = sums_pool.tile([P, CHUNK], F32, name="sums")
                        nc.tensor.matmul_mx(
                            out=sums[:],
                            lhsT=w_codes[:, features].bitcast(FP8X4),
                            lhsT_scale=w_scales[:, features],
                            rhs=codes[:].bitcast(FP8X4),
                            rhs_scale=scales[:],
                            start=True,
                            stop=True,
                        )
                        if block < VECTOR_OUT:
                            nc.scalar.activation(
                                out=h[j][:, block, :],
                                in_=sums[:],
                                func=FUNC.Relu,
                                bias=bias[:, block : block + 1],
                            )
                            nc.vector.bn_stats(out=stats_out[:, block, j, :], in_=h[j][:, block, :])
                        else:
                            nc.scalar.activation(
                                out=h[j][:, block, :],
                                in_=sums[:],
                                func=FUNC.Relu,
                                bias=bias[:, block : block + 1],
                                accum_out=sums_out[:, block - VECTOR_OUT, j : j + 1],
                            )
                    if j == 0:
                        nc.scalar.mul(out=shift_out[:], in_=sums_out[:, :, 0], mul=1.0 / CHUNK)
                    for i in range(SCALAR_OUT):
                        sum_of_squares(
                            h[j][:, VECTOR_OUT + i, :],
                            shift_out[:, i : i + 1],
                            squares_out[:, i, j : j + 1],
                        )

            mean_var_from_records(nc, mean_var_out[:, 0:VECTOR_OUT, :], stats_out)
            total_out = keep.tile([P, SCALAR_OUT], F32, name="total_out")
            nc.vector.reduce_sum(out=total_out[:], in_=sums_out[:], axis=AXIS.X)
            mean_var_from_sums(
                nc,
                keep,
                mean_var_out[:, VECTOR_OUT:, :],
                total_out[:],
                squares_out[:],
                shift_out[:],
                "out",
            )
            scale_out, offset_out = norm_coefficients(
                nc, keep, mean_var_out, params[:, 3 * BLOCKS : 4 * BLOCKS], params[:, 4 * BLOCKS :], "out"
            )

            with tc.tile_pool(name="result", bufs=3) as result_pool, tc.psum_pool(
                name="back", bufs=8
            ) as back_pool:
                for j in range(CHUNKS):
                    for block in range(BLOCKS):
                        nc.vector.tensor_scalar(
                            out=h[j][:, block, :],
                            in0=h[j][:, block, :],
                            scalar1=scale_out[:, block : block + 1],
                            scalar2=offset_out[:, block : block + 1],
                            op0=ALU.mult,
                            op1=ALU.add,
                        )
                    result = result_pool.tile([P, SLICES, D_OUT], F32, name="result")
                    for s in range(SLICES):
                        back = back_pool.tile([P, D_OUT], F32, name="back")
                        for block in range(BLOCKS):
                            nc.tensor.transpose(
                                out=back[:, block * P : (block + 1) * P],
                                in_=h[j][:, block, s * P : (s + 1) * P],
                                identity=ident_f32[:],
                            )
                        if s == SLICES - 1:
                            nc.vector.tensor_copy(out=result[:, s, :], in_=back[:])
                        else:
                            nc.scalar.copy(out=result[:, s, :], in_=back[:])
                    nc.sync.dma_start(
                        out=out_rows[:, j * SLICES : (j + 1) * SLICES, :], in_=result[:]
                    )
